import numpy as np
import ml_dtypes


def mxq(x, axis, fmt="e4m3"):
    dtype, down = {"e4m3": (ml_dtypes.float8_e4m3fn, 7), "e5m2": (ml_dtypes.float8_e5m2, 14)}[fmt]
    v = np.moveaxis(np.asarray(x, np.float32).astype(ml_dtypes.bfloat16).astype(np.float64), axis, -1)
    blocks = v.reshape(v.shape[:-1] + (-1, 32))
    amax = np.abs(blocks).max(-1, keepdims=True)
    byte = np.maximum(np.where(amax > 0, np.frexp(amax)[1] - 1 + 127, 0) - down, 1)
    scale = np.exp2(byte - 127.0)
    codes = (blocks / scale).astype(np.float32).astype(dtype).astype(np.float64)
    return np.moveaxis((codes * scale).reshape(v.shape), -1, axis)


WIDE = False


def mx_kscale(k):
    if not WIDE:
        return np.ones(k)
    levels = np.array([20, -20, 10, -10, 0])
    a = np.random.permutation(np.resize(levels, k // 512 * 4)).reshape(k // 512, 4)
    idx = np.arange(k)
    return np.exp2(a[idx // 512, idx % 128 // 32])


BF16 = ml_dtypes.bfloat16


def bf(x):
    return np.asarray(x, np.float32).astype(BF16)


def f64(x):
    return np.asarray(x).astype(np.float64)


B, L, H = 2, 256, 512
HH = H // 2
BASE = 10000.0


def rope_tables():
    inv_freq = 1.0 / BASE ** (np.arange(0, H, 2) / H)
    freqs = np.outer(np.arange(L), inv_freq)
    emb = np.concatenate([freqs, freqs], axis=-1)
    return np.cos(emb), np.sin(emb)


def rotate_half(x):
    x1, x2 = np.split(x, 2, axis=-1)
    return np.concatenate([-x2, x1], axis=-1)


def rotate_half_t(y):
    y1, y2 = np.split(y, 2, axis=-1)
    return np.concatenate([y2, -y1], axis=-1)


def setup_inputs():
    u = mx_kscale(H)
    cos, sin = rope_tables()
    x = np.random.standard_normal((B, L, H)) * 0.2
    w = np.random.standard_normal((H, H)) * 0.5 / np.sqrt(H) / u[:, None]
    g = np.random.standard_normal((B, L, H)) * np.exp2(np.random.randint(-12, 1, (B, L, 1))) * 16.0 * u
    return {"hidden_states": bf(x), "W_q": bf(w), "cos": bf(cos), "sin": bf(sin), "grad_out": bf(g)}


def reference(hidden_states, W_q, cos, sin, grad_out):
    gh = mxq(f64(grad_out), 2, "e5m2") @ mxq(f64(W_q), 0, "e4m3")
    return gh * f64(cos)[None, :, :] + rotate_half_t(gh * f64(sin)[None, :, :])

@@ -1,0 +1,122 @@
+from contextlib import ExitStack
+
+import concourse.mybir as mybir
+from concourse.masks import make_identity
+
+F32 = mybir.dt.float32
+BF16 = mybir.dt.bfloat16
+U32 = mybir.dt.uint32
+U8 = mybir.dt.uint8
+E4M3X4 = mybir.dt.float8_e4m3fn_x4
+E5M2X4 = mybir.dt.float8_e5m2_x4
+ALU = mybir.AluOpType
+
+P = 128
+PACK = 4
+H = 512
+HALF = H // 2
+SEQ = 256
+TOKENS = 2 * SEQ
+TOKEN_TILES = TOKENS // P
+SEQ_TILES = SEQ // P
+RUN = 4
+W_COLS_VECTOR = 344
+
+FLOPS = 2 * TOKENS * H * H
+BYTES = 2 * (TOKENS * H + H * H + 2 * SEQ * H) + 4 * TOKENS * H
+
+
+def tile_denseattentiononehead_pa_s_kernel(tc, hidden_states, W_q, cos, sin, grad_out, out):
+    nc = tc.nc
+    g_rows = grad_out.flatten_outer_dims()
+    out_rows = out.flatten_outer_dims()
+
+    with ExitStack() as ctx:
+        keep = ctx.enter_context(tc.tile_pool(name="keep", bufs=1))
+        per_tile = ctx.enter_context(tc.tile_pool(name="per_tile", bufs=TOKEN_TILES))
+        per_half = ctx.enter_context(tc.tile_pool(name="per_half", bufs=2 * TOKEN_TILES))
+        psum_turned = ctx.enter_context(tc.psum_pool(name="psum_turned", bufs=TOKEN_TILES))
+        psum_gh = ctx.enter_context(tc.psum_pool(name="psum_gh", bufs=TOKEN_TILES))
+
+        identity = keep.tile([P, P], F32)
+        make_identity(nc, identity[:])
+
+        def load_tokens(n):
+            g_raw = per_tile.tile([P, H], BF16)
+            nc.sync.dma_start(out=g_raw[:], in_=g_rows[n * P : (n + 1) * P, :])
+            return g_raw
+
+        g_raws = [load_tokens(0)]
+        w_raw = keep.tile([P, PACK, H], BF16)
+        nc.sync.dma_start(out=w_raw[:], in_=W_q.rearrange("(p t) j -> p t j", t=PACK))
+        g_raws.append(load_tokens(1))
+        tables = keep.tile([P, SEQ_TILES, 2, H], BF16)
+        nc.sync.dma_start(out=tables[:, :, 0, :], in_=cos.rearrange("(s p) j -> p s j", p=P))
+        nc.sync.dma_start(out=tables[:, :, 1, :], in_=sin.rearrange("(s p) j -> p s j", p=P))
+        g_raws.append(load_tokens(2))
+        g_raws.append(load_tokens(3))
+
+        def quantise_tokens(g_raw):
+            words = g_raw[:].bitcast(F32).rearrange("r (p u) -> r u p", u=2)
+            turned = psum_turned.tile([P, 2, P], F32)
+            for u in range(2):
+                nc.tensor.transpose(turned[:, u, :], words[:, u, :], identity[:])
+            grouped = per_tile.tile([P, P * PACK], BF16, align_bytes=64)
+            nc.scalar.copy(
+                out=grouped[:].bitcast(F32).rearrange("p (r u) -> p r u", u=2),
+                in_=turned[:].rearrange("p u r -> p r u"),
+            )
+            g_codes = per_tile.tile([P, P], U32, align_bytes=64)
+            g_scales = per_tile.tile([P, P], U8, align_bytes=64)
+            nc.vector.quantize_mx(out=g_codes[:].bitcast(E5M2X4), scales=g_scales[:], in_=grouped[:])
+            return g_codes, g_scales
+
+        g_mx = [quantise_tokens(g_raws[0])]
+
+        w_grouped = keep.tile([P, H, PACK], BF16, align_bytes=64)
+
+        def regroup_w(copy, cols):
+            copy(
+                out=w_grouped[:, cols, :].rearrange("p (c i) t -> p c t i", i=RUN),
+                in_=w_raw[:, :, cols].rearrange("p t (c i) -> p c t i", i=RUN),
+            )
+
+        regroup_w(nc.vector.tensor_copy, slice(0, W_COLS_VECTOR))
+        regroup_w(nc.scalar.copy, slice(W_COLS_VECTOR, H))
+        w_codes = keep.tile([P, H], U32, align_bytes=64)
+        w_scales = keep.tile([P, H], U8, align_bytes=64)
+        nc.vector.quantize_mx(
+            out=w_codes[:].bitcast(E4M3X4),
+            scales=w_scales[:],
+            in_=w_grouped[:].rearrange("p j t -> p (j t)"),
+        )
+
+        for n in range(1, TOKEN_TILES):
+            g_mx.append(quantise_tokens(g_raws[n]))
+
+        for n in range(TOKEN_TILES):
+            g_codes, g_scales = g_mx[n]
+            gh = psum_gh.tile([P, H], F32)
+            nc.tensor.matmul_mx(
+                out=gh[:],
+                lhsT=g_codes[:].bitcast(E5M2X4),
+                lhsT_scale=g_scales[:],
+                rhs=w_codes[:].bitcast(E4M3X4),
+                rhs_scale=w_scales[:],
+                start=True,
+                stop=True,
+            )
+            products = per_tile.tile([P, 2, H], F32)
+            nc.vector.tensor_tensor(
+                out=products[:],
+                in0=gh[:].unsqueeze(1).to_broadcast([P, 2, H]),
+                in1=tables[:, n % SEQ_TILES, :, :],
+                op=ALU.mult,
+            )
+            low, high = slice(0, HALF), slice(HALF, H)
+            for mine, other, op in ((low, high, ALU.add), (high, low, ALU.subtract)):
+                rotated = per_half.tile([P, HALF], F32)
+                nc.vector.tensor_tensor(
+                    out=rotated[:], in0=products[:, 0, mine], in1=products[:, 1, other], op=op
+                )
+                nc.sync.dma_start(out=out_rows[n * P : (n + 1) * P, mine], in_=rotated[:])

@@ -113,10 +113,11 @@ def tile_denseattentiononehead_pa_s_kernel(tc, hidden_states, W_q, cos, sin, gra
                 in1=tables[:, n % SEQ_TILES, :, :],
                 op=ALU.mult,
             )
+            summer = nc.gpsimd if n < TOKEN_TILES - 1 else nc.vector
             low, high = slice(0, HALF), slice(HALF, H)
             for mine, other, op in ((low, high, ALU.add), (high, low, ALU.subtract)):
                 rotated = per_half.tile([P, HALF], F32)
-                nc.vector.tensor_tensor(
+                summer.tensor_tensor(
                     out=rotated[:], in0=products[:, 0, mine], in1=products[:, 1, other], op=op
                 )
                 nc.sync.dma_start(out=out_rows[n * P : (n + 1) * P, mine], in_=rotated[:])

@@ -15,63 +15,50 @@ P = 128
 PACK = 4
 H = 512
 HALF = H // 2
+BATCH = 2
 SEQ = 256
-TOKENS = 2 * SEQ
-TOKEN_TILES = TOKENS // P
 SEQ_TILES = SEQ // P
 RUN = 4
 W_COLS_VECTOR = 344
+QUANTISED_AHEAD = 3
 
-FLOPS = 2 * TOKENS * H * H
-BYTES = 2 * (TOKENS * H + H * H + 2 * SEQ * H) + 4 * TOKENS * H
+FLOPS = 2 * BATCH * SEQ * H * H
+BYTES = 2 * (BATCH * SEQ * H + H * H + 2 * SEQ * H) + 4 * BATCH * SEQ * H
 
 
 def tile_denseattentiononehead_pa_s_kernel(tc, hidden_states, W_q, cos, sin, grad_out, out):
     nc = tc.nc
-    g_rows = grad_out.flatten_outer_dims()
-    out_rows = out.flatten_outer_dims()
+    tiles = [(b, s) for b in range(BATCH) for s in range(SEQ_TILES)]
 
     with ExitStack() as ctx:
         keep = ctx.enter_context(tc.tile_pool(name="keep", bufs=1))
-        per_tile = ctx.enter_context(tc.tile_pool(name="per_tile", bufs=TOKEN_TILES))
-        per_half = ctx.enter_context(tc.tile_pool(name="per_half", bufs=2 * TOKEN_TILES))
-        psum_turned = ctx.enter_context(tc.psum_pool(name="psum_turned", bufs=TOKEN_TILES))
-        psum_gh = ctx.enter_context(tc.psum_pool(name="psum_gh", bufs=TOKEN_TILES))
+        per_tile = ctx.enter_context(tc.tile_pool(name="per_tile", bufs=len(tiles)))
+        psum_turned = ctx.enter_context(tc.psum_pool(name="psum_turned", bufs=len(tiles)))
+        psum_gh = ctx.enter_context(tc.psum_pool(name="psum_gh", bufs=len(tiles)))
+        ctx.enter_context(tc.manual_schedule())
 
         identity = keep.tile([P, P], F32)
         make_identity(nc, identity[:])
 
-        def load_tokens(n):
-            g_raw = per_tile.tile([P, H], BF16)
-            nc.sync.dma_start(out=g_raw[:], in_=g_rows[n * P : (n + 1) * P, :])
-            return g_raw
-
-        g_raws = [load_tokens(0)]
         w_raw = keep.tile([P, PACK, H], BF16)
         nc.sync.dma_start(out=w_raw[:], in_=W_q.rearrange("(p t) j -> p t j", t=PACK))
-        g_raws.append(load_tokens(1))
-        tables = keep.tile([P, SEQ_TILES, 2, H], BF16)
-        nc.sync.dma_start(out=tables[:, :, 0, :], in_=cos.rearrange("(s p) j -> p s j", p=P))
-        nc.sync.dma_start(out=tables[:, :, 1, :], in_=sin.rearrange("(s p) j -> p s j", p=P))
-        g_raws.append(load_tokens(2))
-        g_raws.append(load_tokens(3))
 
-        def quantise_tokens(g_raw):
-            words = g_raw[:].bitcast(F32).rearrange("r (p u) -> r u p", u=2)
-            turned = psum_turned.tile([P, 2, P], F32)
-            for u in range(2):
-                nc.tensor.transpose(turned[:, u, :], words[:, u, :], identity[:])
-            grouped = per_tile.tile([P, P * PACK], BF16, align_bytes=64)
-            nc.scalar.copy(
-                out=grouped[:].bitcast(F32).rearrange("p (r u) -> p r u", u=2),
-                in_=turned[:].rearrange("p u r -> p r u"),
+        g_raws = []
+        for b, s in tiles:
+            g_raw = per_tile.tile([P, H], BF16)
+            nc.sync.dma_start(out=g_raw[:], in_=grad_out[b, s * P : (s + 1) * P, :])
+            g_raws.append(g_raw)
+
+        rot = keep.tile([P, SEQ_TILES, 2, 2, HALF], BF16)
+        nc.sync.dma_start(
+            out=rot[:].rearrange("p s x y c -> p s (x y c)")[:, :, HALF : HALF + H],
+            in_=sin.rearrange("(s p) j -> p s j", p=P),
+        )
+        for s in range(SEQ_TILES):
+            nc.sync.dma_start(
+                out=rot[:, s, :, :, :].rearrange("p x y c -> p (x y) c")[:, 0:4:3, :],
+                in_=cos[s * P : (s + 1) * P, :].rearrange("p (x c) -> p x c", x=2),
             )
-            g_codes = per_tile.tile([P, P], U32, align_bytes=64)
-            g_scales = per_tile.tile([P, P], U8, align_bytes=64)
-            nc.vector.quantize_mx(out=g_codes[:].bitcast(E5M2X4), scales=g_scales[:], in_=grouped[:])
-            return g_codes, g_scales
-
-        g_mx = [quantise_tokens(g_raws[0])]
 
         w_grouped = keep.tile([P, H, PACK], BF16, align_bytes=64)
 
@@ -91,10 +78,33 @@ def tile_denseattentiononehead_pa_s_kernel(tc, hidden_states, W_q, cos, sin, gra
             in_=w_grouped[:].rearrange("p j t -> p (j t)"),
         )
 
-        for n in range(1, TOKEN_TILES):
-            g_mx.append(quantise_tokens(g_raws[n]))
+        groupeds = []
+        for g_raw in g_raws:
+            words = g_raw[:].bitcast(F32).rearrange("r (p u) -> r u p", u=2)
+            turned = psum_turned.tile([P, 2, P], F32)
+            for u in range(2):
+                nc.tensor.transpose(turned[:, u, :], words[:, u, :], identity[:])
+            grouped = per_tile.tile([P, P * PACK], BF16, align_bytes=64)
+            nc.scalar.copy(
+                out=grouped[:].bitcast(F32).rearrange("p (r u) -> p r u", u=2),
+                in_=turned[:].rearrange("p u r -> p r u"),
+            )
+            groupeds.append(grouped)
 
-        for n in range(TOKEN_TILES):
+        g_mx = []
+
+        def quantise(n):
+            g_codes = per_tile.tile([P, P], U32, align_bytes=64)
+            g_scales = per_tile.tile([P, P], U8, align_bytes=64)
+            nc.vector.quantize_mx(out=g_codes[:].bitcast(E5M2X4), scales=g_scales[:], in_=groupeds[n][:])
+            g_mx.append((g_codes, g_scales))
+
+        quantise(0)
+        nc.vector.tensor_scalar_mul(out=rot[:, :, 0, 1, :], in0=rot[:, :, 0, 1, :], scalar1=-1.0)
+        for n in range(1, QUANTISED_AHEAD):
+            quantise(n)
+
+        for n, (b, s) in enumerate(tiles):
             g_codes, g_scales = g_mx[n]
             gh = psum_gh.tile([P, H], F32)
             nc.tensor.matmul_mx(
@@ -106,18 +116,25 @@ def tile_denseattentiononehead_pa_s_kernel(tc, hidden_states, W_q, cos, sin, gra
                 start=True,
                 stop=True,
             )
-            products = per_tile.tile([P, 2, H], F32)
+            products = per_tile.tile([P, 2, 2, HALF], F32)
             nc.vector.tensor_tensor(
                 out=products[:],
-                in0=gh[:].unsqueeze(1).to_broadcast([P, 2, H]),
-                in1=tables[:, n % SEQ_TILES, :, :],
+                in0=gh[:].rearrange("p (x c) -> p x c", x=2).unsqueeze(2).to_broadcast([P, 2, 2, HALF]),
+                in1=rot[:, s, :, :, :],
                 op=ALU.mult,
             )
-            summer = nc.gpsimd if n < TOKEN_TILES - 1 else nc.vector
-            low, high = slice(0, HALF), slice(HALF, H)
-            for mine, other, op in ((low, high, ALU.add), (high, low, ALU.subtract)):
-                rotated = per_half.tile([P, HALF], F32)
-                summer.tensor_tensor(
-                    out=rotated[:], in0=products[:, 0, mine], in1=products[:, 1, other], op=op
+            if n + QUANTISED_AHEAD < len(tiles):
+                quantise(n + QUANTISED_AHEAD)
+            rows = out[b, s * P : (s + 1) * P, :].rearrange("p (y c) -> p y c", y=2)
+            rotated = per_tile.tile([P, 2, HALF], F32)
+            if n < len(tiles) - 1:
+                nc.gpsimd.tensor_tensor(
+                    out=rotated[:], in0=products[:, 0, :, :], in1=products[:, 1, :, :], op=ALU.add
                 )
-                nc.sync.dma_start(out=out_rows[n * P : (n + 1) * P, mine], in_=rotated[:])
+                nc.sync.dma_start(out=rows, in_=rotated[:])
+            else:
+                for y in range(2):
+                    nc.vector.tensor_tensor(
+                        out=rotated[:, y, :], in0=products[:, 0, y, :], in1=products[:, 1, y, :], op=ALU.add
+                    )
+                    nc.sync.dma_start(out=rows[:, y, :], in_=rotated[:, y, :])

@@ -20,7 +20,6 @@ SEQ = 256
 SEQ_TILES = SEQ // P
 RUN = 4
 W_COLS_VECTOR = 344
-QUANTISED_AHEAD = 3
 
 FLOPS = 2 * BATCH * SEQ * H * H
 BYTES = 2 * (BATCH * SEQ * H + H * H + 2 * SEQ * H) + 4 * BATCH * SEQ * H
@@ -101,7 +100,7 @@ def tile_denseattentiononehead_pa_s_kernel(tc, hidden_states, W_q, cos, sin, gra
 
         quantise(0)
         nc.vector.tensor_scalar_mul(out=rot[:, :, 0, 1, :], in0=rot[:, :, 0, 1, :], scalar1=-1.0)
-        for n in range(1, QUANTISED_AHEAD):
+        for n in range(1, len(tiles)):
             quantise(n)
 
         for n, (b, s) in enumerate(tiles):
@@ -123,8 +122,6 @@ def tile_denseattentiononehead_pa_s_kernel(tc, hidden_states, W_q, cos, sin, gra
                 in1=rot[:, s, :, :, :],
                 op=ALU.mult,
             )
-            if n + QUANTISED_AHEAD < len(tiles):
-                quantise(n + QUANTISED_AHEAD)
             rows = out[b, s * P : (s + 1) * P, :].rearrange("p (y c) -> p y c", y=2)
             rotated = per_tile.tile([P, 2, HALF], F32)
             if n < len(tiles) - 1:

@@ -20,6 +20,7 @@ SEQ = 256
 SEQ_TILES = SEQ // P
 RUN = 4
 W_COLS_VECTOR = 344
+GPSIMD_HALVES = 5
 
 FLOPS = 2 * BATCH * SEQ * H * H
 BYTES = 2 * (BATCH * SEQ * H + H * H + 2 * SEQ * H) + 4 * BATCH * SEQ * H
@@ -103,6 +104,7 @@ def tile_denseattentiononehead_pa_s_kernel(tc, hidden_states, W_q, cos, sin, gra
         for n in range(1, len(tiles)):
             quantise(n)
 
+        late_halves = []
         for n, (b, s) in enumerate(tiles):
             g_codes, g_scales = g_mx[n]
             gh = psum_gh.tile([P, H], F32)
@@ -124,14 +126,19 @@ def tile_denseattentiononehead_pa_s_kernel(tc, hidden_states, W_q, cos, sin, gra
             )
             rows = out[b, s * P : (s + 1) * P, :].rearrange("p (y c) -> p y c", y=2)
             rotated = per_tile.tile([P, 2, HALF], F32)
-            if n < len(tiles) - 1:
+            early = min(2, max(0, GPSIMD_HALVES - 2 * n))
+            if early > 0:
                 nc.gpsimd.tensor_tensor(
-                    out=rotated[:], in0=products[:, 0, :, :], in1=products[:, 1, :, :], op=ALU.add
+                    out=rotated[:, :early, :],
+                    in0=products[:, 0, :early, :],
+                    in1=products[:, 1, :early, :],
+                    op=ALU.add,
                 )
-                nc.sync.dma_start(out=rows, in_=rotated[:])
-            else:
-                for y in range(2):
-                    nc.vector.tensor_tensor(
-                        out=rotated[:, y, :], in0=products[:, 0, y, :], in1=products[:, 1, y, :], op=ALU.add
-                    )
-                    nc.sync.dma_start(out=rows[:, y, :], in_=rotated[:, y, :])
+                nc.sync.dma_start(out=rows[:, :early, :], in_=rotated[:, :early, :])
+            late_halves.extend((products, rotated, rows, y) for y in range(early, 2))
+
+        for products, rotated, rows, y in late_halves:
+            nc.vector.tensor_tensor(
+                out=rotated[:, y, :], in0=products[:, 0, y, :], in1=products[:, 1, y, :], op=ALU.add
+            )
+            nc.sync.dma_start(out=rows[:, y, :], in_=rotated[:, y, :])

@@ -21,6 +21,7 @@ SEQ_TILES = SEQ // P
 RUN = 4
 W_COLS_VECTOR = 344
 GPSIMD_HALVES = 5
+WARM_MATMULS = 3
 
 FLOPS = 2 * BATCH * SEQ * H * H
 BYTES = 2 * (BATCH * SEQ * H + H * H + 2 * SEQ * H) + 4 * BATCH * SEQ * H
@@ -28,7 +29,7 @@ BYTES = 2 * (BATCH * SEQ * H + H * H + 2 * SEQ * H) + 4 * BATCH * SEQ * H
 
 def tile_denseattentiononehead_pa_s_kernel(tc, hidden_states, W_q, cos, sin, grad_out, out):
     nc = tc.nc
-    tiles = [(b, s) for b in range(BATCH) for s in range(SEQ_TILES)]
+    tiles = [(b, s) for s in range(SEQ_TILES) for b in range(BATCH)]
 
     with ExitStack() as ctx:
         keep = ctx.enter_context(tc.tile_pool(name="keep", bufs=1))
@@ -37,11 +38,27 @@ def tile_denseattentiononehead_pa_s_kernel(tc, hidden_states, W_q, cos, sin, gra
         psum_gh = ctx.enter_context(tc.psum_pool(name="psum_gh", bufs=len(tiles)))
         ctx.enter_context(tc.manual_schedule())
 
+        zero = keep.tile([P, 1], F32)
+        nc.vector.memset(zero[:], 0.0)
+        unused = keep.tile([P, 1], F32)
+        nc.scalar.copy(out=unused[:], in_=zero[:])
+
+        idle_in = keep.tile([P, HALF], F32)
+        nc.vector.memset(idle_in[:], 0.0)
+        for i in range(WARM_MATMULS):
+            turned = psum_turned.tile([P, 2, P], F32)
+            nc.tensor.matmul(
+                out=turned[:].rearrange("p u r -> p (u r)"), lhsT=idle_in[:, :P], rhs=idle_in[:], start=True, stop=True
+            )
+
         identity = keep.tile([P, P], F32)
         make_identity(nc, identity[:])
 
-        w_raw = keep.tile([P, PACK, H], BF16)
-        nc.sync.dma_start(out=w_raw[:], in_=W_q.rearrange("(p t) j -> p t j", t=PACK))
+        w_raws = []
+        for u in range(2):
+            w_raw = keep.tile([P, 2, H], BF16, name="w_raw%d" % u)
+            nc.sync.dma_start(out=w_raw[:], in_=W_q[HALF * u : HALF * (u + 1), :].rearrange("(p e) j -> p e j", e=2))
+            w_raws.append(w_raw)
 
         g_raws = []
         for b, s in tiles:
@@ -50,11 +67,11 @@ def tile_denseattentiononehead_pa_s_kernel(tc, hidden_states, W_q, cos, sin, gra
             g_raws.append(g_raw)
 
         rot = keep.tile([P, SEQ_TILES, 2, 2, HALF], BF16)
-        nc.sync.dma_start(
-            out=rot[:].rearrange("p s x y c -> p s (x y c)")[:, :, HALF : HALF + H],
-            in_=sin.rearrange("(s p) j -> p s j", p=P),
-        )
         for s in range(SEQ_TILES):
+            nc.sync.dma_start(
+                out=rot[:, s, :, :, :].rearrange("p x y c -> p (x y c)")[:, HALF : HALF + H],
+                in_=sin[s * P : (s + 1) * P, :],
+            )
             nc.sync.dma_start(
                 out=rot[:, s, :, :, :].rearrange("p x y c -> p (x y) c")[:, 0:4:3, :],
                 in_=cos[s * P : (s + 1) * P, :].rearrange("p (x c) -> p x c", x=2),
@@ -62,14 +79,15 @@ def tile_denseattentiononehead_pa_s_kernel(tc, hidden_states, W_q, cos, sin, gra
 
         w_grouped = keep.tile([P, H, PACK], BF16, align_bytes=64)
 
-        def regroup_w(copy, cols):
+        def regroup_w(copy, u, cols):
             copy(
-                out=w_grouped[:, cols, :].rearrange("p (c i) t -> p c t i", i=RUN),
-                in_=w_raw[:, :, cols].rearrange("p t (c i) -> p c t i", i=RUN),
+                out=w_grouped[:, cols, 2 * u : 2 * u + 2].rearrange("p (c i) e -> p c e i", i=RUN),
+                in_=w_raws[u][:, :, cols].rearrange("p e (c i) -> p c e i", i=RUN),
             )
 
-        regroup_w(nc.vector.tensor_copy, slice(0, W_COLS_VECTOR))
-        regroup_w(nc.scalar.copy, slice(W_COLS_VECTOR, H))
+        for u in range(2):
+            regroup_w(nc.vector.tensor_copy, u, slice(0, W_COLS_VECTOR))
+            regroup_w(nc.scalar.copy, u, slice(W_COLS_VECTOR, H))
         w_codes = keep.tile([P, H], U32, align_bytes=64)
         w_scales = keep.tile([P, H], U8, align_bytes=64)
         nc.vector.quantize_mx(
@@ -80,7 +98,7 @@ def tile_denseattentiononehead_pa_s_kernel(tc, hidden_states, W_q, cos, sin, gra
 
         groupeds = []
         for g_raw in g_raws:
-            words = g_raw[:].bitcast(F32).rearrange("r (p u) -> r u p", u=2)
+            words = g_raw[:].bitcast(F32).rearrange("r (u p) -> r u p", u=2)
             turned = psum_turned.tile([P, 2, P], F32)
             for u in range(2):
                 nc.tensor.transpose(turned[:, u, :], words[:, u, :], identity[:])
@@ -90,6 +108,7 @@ def tile_denseattentiononehead_pa_s_kernel(tc, hidden_states, W_q, cos, sin, gra
                 in_=turned[:].rearrange("p u r -> p r u"),
             )
             groupeds.append(grouped)
+        nc.scalar.mul(out=rot[:, 0, 0, 1, :], in_=rot[:, 0, 0, 1, :], mul=-1.0)
 
         g_mx = []
 
@@ -99,9 +118,7 @@ def tile_denseattentiononehead_pa_s_kernel(tc, hidden_states, W_q, cos, sin, gra
             nc.vector.quantize_mx(out=g_codes[:].bitcast(E5M2X4), scales=g_scales[:], in_=groupeds[n][:])
             g_mx.append((g_codes, g_scales))
 
-        quantise(0)
-        nc.vector.tensor_scalar_mul(out=rot[:, :, 0, 1, :], in0=rot[:, :, 0, 1, :], scalar1=-1.0)
-        for n in range(1, len(tiles)):
+        for n in range(len(tiles)):
             quantise(n)
 
         late_halves = []
@@ -135,10 +152,14 @@ def tile_denseattentiononehead_pa_s_kernel(tc, hidden_states, W_q, cos, sin, gra
                     op=ALU.add,
                 )
                 nc.sync.dma_start(out=rows[:, :early, :], in_=rotated[:, :early, :])
-            late_halves.extend((products, rotated, rows, y) for y in range(early, 2))
+            assert s == 0 or early < 2
+            late_halves.extend((products, rotated, rows, y, s) for y in range(early, 2))
 
-        for products, rotated, rows, y in late_halves:
+        for products, rotated, rows, y, s in late_halves:
             nc.vector.tensor_tensor(
-                out=rotated[:, y, :], in0=products[:, 0, y, :], in1=products[:, 1, y, :], op=ALU.add
+                out=rotated[:, y, :],
+                in0=products[:, 1, y, :],
+                in1=products[:, 0, y, :],
+                op=ALU.subtract if (s > 0 and y == 1) else ALU.add,
             )
             nc.sync.dma_start(out=rows[:, y, :], in_=rotated[:, y, :])

@@ -85,16 +85,19 @@ def tile_denseattentiononehead_pa_s_kernel(tc, hidden_states, W_q, cos, sin, gra
                 in_=w_raws[u][:, :, cols].rearrange("p e (c i) -> p c e i", i=RUN),
             )
 
-        for u in range(2):
-            regroup_w(nc.vector.tensor_copy, u, slice(0, W_COLS_VECTOR))
-            regroup_w(nc.scalar.copy, u, slice(W_COLS_VECTOR, H))
+        regroup_w(nc.vector.tensor_copy, 0, slice(0, W_COLS_VECTOR))
+        regroup_w(nc.scalar.copy, 0, slice(W_COLS_VECTOR, H))
+        regroup_w(nc.vector.tensor_copy, 1, slice(HALF, W_COLS_VECTOR))
+        regroup_w(nc.vector.tensor_copy, 1, slice(0, HALF))
+        regroup_w(nc.scalar.copy, 1, slice(W_COLS_VECTOR, H))
         w_codes = keep.tile([P, H], U32, align_bytes=64)
         w_scales = keep.tile([P, H], U8, align_bytes=64)
-        nc.vector.quantize_mx(
-            out=w_codes[:].bitcast(E4M3X4),
-            scales=w_scales[:],
-            in_=w_grouped[:].rearrange("p j t -> p (j t)"),
-        )
+        for h in (1, 0):
+            nc.vector.quantize_mx(
+                out=w_codes[:, h * HALF : (h + 1) * HALF].bitcast(E4M3X4),
+                scales=w_scales[:, h * HALF : (h + 1) * HALF],
+                in_=w_grouped[:, h * HALF : (h + 1) * HALF, :].rearrange("p j t -> p (j t)"),
+            )
 
         groupeds = []
         for g_raw in g_raws:

@@ -111,7 +111,6 @@ def tile_denseattentiononehead_pa_s_kernel(tc, hidden_states, W_q, cos, sin, gra
                 in_=turned[:].rearrange("p u r -> p r u"),
             )
             groupeds.append(grouped)
-        nc.scalar.mul(out=rot[:, 0, 0, 1, :], in_=rot[:, 0, 0, 1, :], mul=-1.0)
 
         g_mx = []
 
@@ -122,6 +121,8 @@ def tile_denseattentiononehead_pa_s_kernel(tc, hidden_states, W_q, cos, sin, gra
             g_mx.append((g_codes, g_scales))
 
         for n in range(len(tiles)):
+            if n == len(tiles) - 1:
+                nc.vector.tensor_scalar_mul(out=rot[:, 0, 0, 1, :], in0=rot[:, 0, 0, 1, :], scalar1=-1.0)
             quantise(n)
 
         late_halves = []

from contextlib import ExitStack

import concourse.mybir as mybir
from concourse.masks import make_identity

F32 = mybir.dt.float32
BF16 = mybir.dt.bfloat16
U32 = mybir.dt.uint32
U8 = mybir.dt.uint8
E4M3X4 = mybir.dt.float8_e4m3fn_x4
E5M2X4 = mybir.dt.float8_e5m2_x4
ALU = mybir.AluOpType

P = 128
PACK = 4
H = 512
HALF = H // 2
BATCH = 2
SEQ = 256
SEQ_TILES = SEQ // P
RUN = 4
W_COLS_VECTOR = 344
GPSIMD_HALVES = 5
WARM_MATMULS = 3

FLOPS = 2 * BATCH * SEQ * H * H
BYTES = 2 * (BATCH * SEQ * H + H * H + 2 * SEQ * H) + 4 * BATCH * SEQ * H


def tile_denseattentiononehead_pa_s_kernel(tc, hidden_states, W_q, cos, sin, grad_out, out):
    nc = tc.nc
    tiles = [(b, s) for s in range(SEQ_TILES) for b in range(BATCH)]

    with ExitStack() as ctx:
        keep = ctx.enter_context(tc.tile_pool(name="keep", bufs=1))
        per_tile = ctx.enter_context(tc.tile_pool(name="per_tile", bufs=len(tiles)))
        psum_turned = ctx.enter_context(tc.psum_pool(name="psum_turned", bufs=len(tiles)))
        psum_gh = ctx.enter_context(tc.psum_pool(name="psum_gh", bufs=len(tiles)))
        ctx.enter_context(tc.manual_schedule())

        zero = keep.tile([P, 1], F32)
        nc.vector.memset(zero[:], 0.0)
        unused = keep.tile([P, 1], F32)
        nc.scalar.copy(out=unused[:], in_=zero[:])

        idle_in = keep.tile([P, HALF], F32)
        nc.vector.memset(idle_in[:], 0.0)
        for i in range(WARM_MATMULS):
            turned = psum_turned.tile([P, 2, P], F32)
            nc.tensor.matmul(
                out=turned[:].rearrange("p u r -> p (u r)"), lhsT=idle_in[:, :P], rhs=idle_in[:], start=True, stop=True
            )

        identity = keep.tile([P, P], F32)
        make_identity(nc, identity[:])

        w_raws = []
        for u in range(2):
            w_raw = keep.tile([P, 2, H], BF16, name="w_raw%d" % u)
            nc.sync.dma_start(out=w_raw[:], in_=W_q[HALF * u : HALF * (u + 1), :].rearrange("(p e) j -> p e j", e=2))
            w_raws.append(w_raw)

        g_raws = []
        for b, s in tiles:
            g_raw = per_tile.tile([P, H], BF16)
            nc.sync.dma_start(out=g_raw[:], in_=grad_out[b, s * P : (s + 1) * P, :])
            g_raws.append(g_raw)

        rot = keep.tile([P, SEQ_TILES, 2, 2, HALF], BF16)
        for s in range(SEQ_TILES):
            nc.sync.dma_start(
                out=rot[:, s, :, :, :].rearrange("p x y c -> p (x y c)")[:, HALF : HALF + H],
                in_=sin[s * P : (s + 1) * P, :],
            )
            nc.sync.dma_start(
                out=rot[:, s, :, :, :].rearrange("p x y c -> p (x y) c")[:, 0:4:3, :],
                in_=cos[s * P : (s + 1) * P, :].rearrange("p (x c) -> p x c", x=2),
            )

        w_grouped = keep.tile([P, H, PACK], BF16, align_bytes=64)

        def regroup_w(copy, u, cols):
            copy(
                out=w_grouped[:, cols, 2 * u : 2 * u + 2].rearrange("p (c i) e -> p c e i", i=RUN),
                in_=w_raws[u][:, :, cols].rearrange("p e (c i) -> p c e i", i=RUN),
            )

        regroup_w(nc.vector.tensor_copy, 0, slice(0, W_COLS_VECTOR))
        regroup_w(nc.scalar.copy, 0, slice(W_COLS_VECTOR, H))
        regroup_w(nc.vector.tensor_copy, 1, slice(HALF, W_COLS_VECTOR))
        regroup_w(nc.vector.tensor_copy, 1, slice(0, HALF))
        regroup_w(nc.scalar.copy, 1, slice(W_COLS_VECTOR, H))
        w_codes = keep.tile([P, H], U32, align_bytes=64)
        w_scales = keep.tile([P, H], U8, align_bytes=64)
        for h in (1, 0):
            nc.vector.quantize_mx(
                out=w_codes[:, h * HALF : (h + 1) * HALF].bitcast(E4M3X4),
                scales=w_scales[:, h * HALF : (h + 1) * HALF],
                in_=w_grouped[:, h * HALF : (h + 1) * HALF, :].rearrange("p j t -> p (j t)"),
            )

        groupeds = []
        for g_raw in g_raws:
            words = g_raw[:].bitcast(F32).rearrange("r (u p) -> r u p", u=2)
            turned = psum_turned.tile([P, 2, P], F32)
            for u in range(2):
                nc.tensor.transpose(turned[:, u, :], words[:, u, :], identity[:])
            grouped = per_tile.tile([P, P * PACK], BF16, align_bytes=64)
            nc.scalar.copy(
                out=grouped[:].bitcast(F32).rearrange("p (r u) -> p r u", u=2),
                in_=turned[:].rearrange("p u r -> p r u"),
            )
            groupeds.append(grouped)

        g_mx = []

        def quantise(n):
            g_codes = per_tile.tile([P, P], U32, align_bytes=64)
            g_scales = per_tile.tile([P, P], U8, align_bytes=64)
            nc.vector.quantize_mx(out=g_codes[:].bitcast(E5M2X4), scales=g_scales[:], in_=groupeds[n][:])
            g_mx.append((g_codes, g_scales))

        for n in range(len(tiles)):
            if n == len(tiles) - 1:
                nc.vector.tensor_scalar_mul(out=rot[:, 0, 0, 1, :], in0=rot[:, 0, 0, 1, :], scalar1=-1.0)
            quantise(n)

        late_halves = []
        for n, (b, s) in enumerate(tiles):
            g_codes, g_scales = g_mx[n]
            gh = psum_gh.tile([P, H], F32)
            nc.tensor.matmul_mx(
                out=gh[:],
                lhsT=g_codes[:].bitcast(E5M2X4),
                lhsT_scale=g_scales[:],
                rhs=w_codes[:].bitcast(E4M3X4),
                rhs_scale=w_scales[:],
                start=True,
                stop=True,
            )
            products = per_tile.tile([P, 2, 2, HALF], F32)
            nc.vector.tensor_tensor(
                out=products[:],
                in0=gh[:].rearrange("p (x c) -> p x c", x=2).unsqueeze(2).to_broadcast([P, 2, 2, HALF]),
                in1=rot[:, s, :, :, :],
                op=ALU.mult,
            )
            rows = out[b, s * P : (s + 1) * P, :].rearrange("p (y c) -> p y c", y=2)
            rotated = per_tile.tile([P, 2, HALF], F32)
            early = min(2, max(0, GPSIMD_HALVES - 2 * n))
            if early > 0:
                nc.gpsimd.tensor_tensor(
                    out=rotated[:, :early, :],
                    in0=products[:, 0, :early, :],
                    in1=products[:, 1, :early, :],
                    op=ALU.add,
                )
                nc.sync.dma_start(out=rows[:, :early, :], in_=rotated[:, :early, :])
            assert s == 0 or early < 2
            late_halves.extend((products, rotated, rows, y, s) for y in range(early, 2))

        for products, rotated, rows, y, s in late_halves:
            nc.vector.tensor_tensor(
                out=rotated[:, y, :],
                in0=products[:, 1, y, :],
                in1=products[:, 0, y, :],
                op=ALU.subtract if (s > 0 and y == 1) else ALU.add,
            )
            nc.sync.dma_start(out=rows[:, y, :], in_=rotated[:, y, :])
